import numpy as np
import ml_dtypes


def mxq(x, axis, fmt="e4m3"):
    dtype, down = {"e4m3": (ml_dtypes.float8_e4m3fn, 7), "e5m2": (ml_dtypes.float8_e5m2, 14)}[fmt]
    v = np.moveaxis(np.asarray(x, np.float32).astype(ml_dtypes.bfloat16).astype(np.float64), axis, -1)
    blocks = v.reshape(v.shape[:-1] + (-1, 32))
    amax = np.abs(blocks).max(-1, keepdims=True)
    byte = np.maximum(np.where(amax > 0, np.frexp(amax)[1] - 1 + 127, 0) - down, 1)
    scale = np.exp2(byte - 127.0)
    codes = (blocks / scale).astype(np.float32).astype(dtype).astype(np.float64)
    return np.moveaxis((codes * scale).reshape(v.shape), -1, axis)


WIDE = False


def mx_kscale(k):
    if not WIDE:
        return np.ones(k)
    levels = np.array([10, -10, 5, -5, 0])
    a = np.random.permutation(np.resize(levels, k // 512 * 4)).reshape(k // 512, 4)
    idx = np.arange(k)
    return np.exp2(a[idx // 512, idx % 128 // 32])


BF16 = ml_dtypes.bfloat16


def bf(x):
    return np.asarray(x, np.float32).astype(BF16)


def f64(x):
    return np.asarray(x).astype(np.float64)


N, DIN, DOUT = 1024, 1024, 1024
EPS = 1e-7


def artanh(v):
    return 0.5 * np.log((1.0 + v) / (1.0 - v))


def logmap0(p):
    n = np.sqrt(np.sum(p * p, axis=-1, keepdims=True))
    n_safe = np.clip(n, EPS, 1.0 - EPS)
    return artanh(n_safe) * p / n_safe


def expmap0(v):
    n = np.sqrt(np.sum(v * v, axis=-1, keepdims=True))
    n_safe = np.maximum(n, EPS)
    return np.tanh(n_safe) * v / n_safe


def setup_inputs():
    s = mx_kscale(DIN)
    c = np.sqrt(np.mean(s * s))
    g = np.random.standard_normal((N, DIN)) * s
    rad = 0.1 + 0.4 * np.random.random((N, 1))
    mid = rad * g / np.sqrt(np.sum(g * g, axis=1, keepdims=True))
    return {"mid": bf(mid),
            "W": bf(np.random.standard_normal((DIN, DOUT)) * 4.0 / np.sqrt(DOUT) * c / s[:, None]),
            "b": bf(np.random.standard_normal(DOUT) * 0.7 / np.sqrt(DOUT))}


def reference(mid, W, b):
    u = logmap0(f64(mid))
    y = np.maximum((mxq(u, 1, "e4m3") @ mxq(f64(W), 0, "e4m3")) + f64(b), 0.0)
    return expmap0(y)

@@ -1,0 +1,260 @@
+from contextlib import ExitStack
+
+import concourse.mybir as mybir
+from concourse.masks import make_identity
+
+FLOPS = 2 * 1024 * 1024 * 1024
+
+F32 = mybir.dt.float32
+BF16 = mybir.dt.bfloat16
+U32 = mybir.dt.uint32
+U8 = mybir.dt.uint8
+FP8X4 = mybir.dt.float8_e4m3fn_x4
+ALU = mybir.AluOpType
+ACT = mybir.ActivationFunctionType
+
+P = 128
+HALF = 512
+EPS = 1e-7
+SS_LO = EPS * EPS
+SS_HI = (1.0 - EPS) * (1.0 - EPS)
+BIG = 3.0e38
+
+ORDER = [["v_ms",0],["g_id",0],["ld_mid",0],["s_dummy",0],["ld_b",0],["ld_w",0],["ld_mid",1],["pe_b",0],["ld_w",1],["sq",0],["bcp",0],["ld_mid",2],["wr",0],["ga",0],["ld_w",2],["sq",1],["ld_mid",3],["wr",1],["ln",0],["ga",1],["ld_w",3],["sq",2],["wq",0],["ld_mid",4],["f",0],["wr",2],["ga",2],["ld_mid",5],["sq",3],["ld_mid",6],["wq",2],["ld_mid",7],["ln",1],["ln",2],["ga",3],["bcp",1],["sq",4],["d",0],["wr",3],["tr",0],["ln",3],["sq",6],["ga",4],["f",1],["f",3],["wq",1],["sq",5],["f",2],["ga",6],["d",3],["d",2],["wq",3],["tr",2],["ln",4],["cp",0],["ga",5],["f",4],["d",1],["d",4],["tr",1],["ln",6],["uq",0],["ln",5],["cp",1],["f",5],["f",6],["d",5],["mx",0],["d",6],["cp",2],["uq",1],["tr",3],["pa",0],["mx",1],["sq",7],["uq",2],["pb",0],["cp",3],["mx",2],["ga",7],["pa",1],["tr",4],["gb",0],["ln",7],["tr",5],["f",7],["pa",2],["tr",6],["cp",5],["uq",3],["cp",6],["d",7],["pb",1],["tr",7],["cp",4],["mx",3],["pb",2],["gb",1],["th",0],["uq",4],["gb",2],["uq",5],["uq",6],["mx",4],["pa",3],["cp",7],["gm",0],["pa",4],["mx",5],["pc",0],["pb",3],["mx",6],["th",2],["th",1],["st",0],["gm",2],["gm",1],["uq",7],["gb",3],["pa",5],["th",3],["gm",3],["pb",5],["mx",7],["pc",3],["pb",4],["gb",5],["pc",1],["pa",6],["gb",4],["th",5],["pc",2],["st",1],["gm",5],["pb",6],["th",4],["st",2],["gm",4],["pc",4],["pa",7],["gb",6],["st",3],["th",6],["pc",5],["pb",7],["st",4],["gm",6],["pc",6],["st",5],["gb",7],["th",7],["st",6],["gm",7],["pc",7],["st",7]]
+PINNED = True
+CP_V = []
+P2_S = []
+P3_V = []
+
+
+def tile_graphconvhyp_pb_kernel(tc, mid, W, b, out):
+    nc = tc.nc
+    with ExitStack() as ctx:
+        const = ctx.enter_context(tc.tile_pool(name="const", bufs=1))
+        midp = ctx.enter_context(tc.tile_pool(name="midp", bufs=8))
+        wrawp = ctx.enter_context(tc.tile_pool(name="wrawp", bufs=4))
+        wgrpp = ctx.enter_context(tc.tile_pool(name="wgrpp", bufs=4))
+        up = ctx.enter_context(tc.tile_pool(name="up", bufs=8))
+        ugp = ctx.enter_context(tc.tile_pool(name="ugp", bufs=8))
+        junk = ctx.enter_context(tc.tile_pool(name="junk", bufs=2))
+        tp = ctx.enter_context(tc.tile_pool(name="tp", bufs=8))
+        small = ctx.enter_context(tc.tile_pool(name="small", bufs=8))
+        pst = ctx.enter_context(tc.psum_pool(name="pst", bufs=4))
+        psa = ctx.enter_context(tc.psum_pool(name="psa", bufs=4))
+        if PINNED:
+            ctx.enter_context(tc.manual_schedule())
+
+        ident = const.tile([P, P], BF16, name="ident")
+        ones = const.tile([P, P], BF16, name="ones")
+        brow = const.tile([P, 1024], BF16, name="brow")
+        b_bc = const.tile([P, 1024], BF16, name="b_bc")
+        expo = const.tile([P, 2], F32, name="expo")
+        sgn = const.tile([P, 2], F32, name="sgn")
+        dm_in = const.tile([P, 1], F32, name="dm_in")
+        dm_out = const.tile([P, 1], F32, name="dm_out")
+        wcodes = const.tile([P, 2, 1024], U32, name="wcodes", align_bytes=64)
+        wscales = const.tile([P, 2, 1024], U8, name="wscales", align_bytes=64)
+        ucodes = const.tile([P, 8, 256], U32, name="ucodes", align_bytes=64)
+        uscales = const.tile([P, 8, 256], U8, name="uscales", align_bytes=64)
+
+        st = {}
+
+        def op_v_ms(i):
+            nc.vector.memset(dm_in[:], 1.0)
+            nc.vector.memset(brow[:], 0.0)
+            nc.vector.memset(ones[:], 1.0)
+
+        def op_g_id(i):
+            nc.gpsimd.memset(expo[:, 0:1], 0.5)
+            nc.gpsimd.memset(expo[:, 1:2], -0.5)
+            nc.gpsimd.memset(sgn[:, 0:1], 1.0)
+            nc.gpsimd.memset(sgn[:, 1:2], -1.0)
+            make_identity(nc, ident[:])
+
+        def op_s_dummy(i):
+            nc.scalar.activation(out=dm_out[:], in_=dm_in[:], func=ACT.Ln)
+
+        def op_ld_b(i):
+            nc.scalar.dma_start(out=brow[0:1, :], in_=b.rearrange("(o n) -> o n", o=1))
+
+        def op_ld_mid(i):
+            mt = midp.tile([P, 1024], BF16, name="mt", tag="mt")
+            st[("mt", i)] = mt
+            nc.sync.dma_start(out=mt[:], in_=mid[i * P:(i + 1) * P, :])
+
+        def op_ld_w(j):
+            g, nh = divmod(j, 2)
+            wr = wrawp.tile([P, 4, HALF], BF16, name="wr", tag="wr")
+            st[("wr", j)] = wr
+            nc.sync.dma_start(
+                out=wr[:],
+                in_=W[g * 512:(g + 1) * 512, nh * HALF:(nh + 1) * HALF].rearrange(
+                    "(t p) n -> p t n", t=4, p=P
+                ),
+            )
+
+        def op_pe_b(i):
+            for nh in range(2):
+                pb = psa.tile([P, HALF], F32, name="pb", tag="acc")
+                st[("pbias", nh)] = pb
+                nc.tensor.matmul(
+                    out=pb[:], lhsT=ones[:], rhs=brow[:, nh * HALF:(nh + 1) * HALF],
+                    start=True, stop=True,
+                )
+
+        def op_bcp(nh):
+            nc.vector.tensor_copy(out=b_bc[:, nh * HALF:(nh + 1) * HALF], in_=st[("pbias", nh)][:])
+
+        def op_sq(i):
+            sj = junk.tile([P, 1024], BF16, name="sj", tag="sj")
+            ss = small.tile([P, 1], F32, name="ss", tag="ss")
+            st[("ss", i)] = ss
+            nc.scalar.activation(out=sj[:], in_=st[("mt", i)][:], func=ACT.Square, accum_out=ss[:])
+
+        def op_ga(i):
+            ssc = small.tile([P, 1], F32, name="ssc", tag="ssc")
+            nr = small.tile([P, 2], F32, name="nr", tag="nr")
+            pm = small.tile([P, 2], F32, name="pm", tag="pm")
+            st[("nr", i)] = nr
+            st[("pm", i)] = pm
+            nc.gpsimd.tensor_scalar(out=ssc[:], in0=st[("ss", i)][:], scalar1=SS_HI, scalar2=SS_LO,
+                                    op0=ALU.min, op1=ALU.max)
+            nc.gpsimd.tensor_tensor(out=nr[:], in0=ssc[:, 0:1].to_broadcast([P, 2]), in1=expo[:], op=ALU.pow)
+            nc.gpsimd.tensor_scalar(out=pm[:], in0=sgn[:], scalar1=nr[:, 0:1], scalar2=1.0,
+                                    op0=ALU.mult, op1=ALU.add)
+
+        def op_ln(i):
+            lg = small.tile([P, 2], F32, name="lg", tag="lg")
+            st[("lg", i)] = lg
+            nc.scalar.activation(out=lg[:], in_=st[("pm", i)][:], func=ACT.Ln)
+
+        def op_f(i):
+            f2 = small.tile([P, 1], F32, name="f2", tag="f2")
+            st[("f2", i)] = f2
+            lg = st[("lg", i)]
+            nc.vector.scalar_tensor_tensor(out=f2[:], in0=lg[:, 0:1], scalar=lg[:, 1:2],
+                                           in1=st[("nr", i)][:, 1:2], op0=ALU.subtract, op1=ALU.mult)
+
+        def op_d(i):
+            u = up.tile([P, 1024], BF16, name="u", tag="u")
+            st[("u", i)] = u
+            nc.vector.tensor_scalar(out=u[:], in0=st[("mt", i)][:], scalar1=st[("f2", i)][:, 0:1],
+                                    scalar2=0.5, op0=ALU.mult, op1=ALU.mult)
+
+        def op_tr(i):
+            xt = pst.tile([P, 2, 4, P], BF16, name="xt", tag="xt")
+            st[("xt", i)] = xt
+            u = st[("u", i)]
+            for g in range(2):
+                for t in range(4):
+                    c0 = (g * 4 + t) * P
+                    nc.tensor.transpose(xt[:, g, t, :], u[:, c0:c0 + P], ident[:])
+
+        def op_cp(i):
+            ug = ugp.tile([P, 2, P, 4], BF16, name="ug", tag="ug", align_bytes=64)
+            st[("ug", i)] = ug
+            src = st[("xt", i)][:].rearrange("p g t r -> p g r t")
+            if i in CP_V:
+                nc.vector.tensor_copy(out=ug[:], in_=src)
+            else:
+                nc.scalar.copy(out=ug[:], in_=src)
+
+        def op_uq(i):
+            nc.vector.quantize_mx(
+                out=ucodes[:, i, :].bitcast(FP8X4),
+                scales=uscales[:, i, :],
+                in_=st[("ug", i)][:].rearrange("p g r t -> p (g r t)"),
+            )
+
+        def op_wr(j):
+            wg = wgrpp.tile([P, HALF, 4], BF16, name="wg", tag="wg", align_bytes=64)
+            st[("wg", j)] = wg
+            nc.vector.tensor_copy(
+                out=wg[:].rearrange("p (c i) t -> p c t i", i=4),
+                in_=st[("wr", j)][:].rearrange("p t (c i) -> p c t i", i=4),
+            )
+
+        def op_wq(j):
+            g, nh = divmod(j, 2)
+            nc.vector.quantize_mx(
+                out=wcodes[:, g, nh * HALF:(nh + 1) * HALF].bitcast(FP8X4),
+                scales=wscales[:, g, nh * HALF:(nh + 1) * HALF],
+                in_=st[("wg", j)][:].rearrange("p n t -> p (n t)"),
+            )
+
+        def op_mx(i):
+            for nh in range(2):
+                acc = psa.tile([P, HALF], F32, name="acc", tag="acc")
+                st[("acc", i, nh)] = acc
+                for g in range(2):
+                    nc.tensor.matmul_mx(
+                        out=acc[:],
+                        lhsT=ucodes[:, i, g * P:(g + 1) * P].bitcast(FP8X4),
+                        lhsT_scale=uscales[:, i, g * P:(g + 1) * P],
+                        rhs=wcodes[:, g, nh * HALF:(nh + 1) * HALF].bitcast(FP8X4),
+                        rhs_scale=wscales[:, g, nh * HALF:(nh + 1) * HALF],
+                        start=(g == 0),
+                        stop=(g == 1),
+                    )
+
+        def op_pa(i):
+            t = tp.tile([P, 1024], F32, name="t", tag="t")
+            st[("t", i)] = t
+            for nh in range(2):
+                nc.vector.tensor_tensor(out=t[:, nh * HALF:(nh + 1) * HALF], in0=st[("acc", i, nh)][:],
+                                        in1=b_bc[:, nh * HALF:(nh + 1) * HALF], op=ALU.add)
+
+        def op_rl(i):
+            t = st[("t", i)]
+            nc.scalar.activation(out=t[:], in_=t[:], func=ACT.Relu)
+
+        def op_pb(i):
+            t = st[("t", i)]
+            j2 = junk.tile([P, 1024], F32, name="j2", tag="j2")
+            sy = small.tile([P, 1], F32, name="sy", tag="sy")
+            st[("sy", i)] = sy
+            if i in P2_S:
+                nc.scalar.activation(out=j2[:], in_=t[:], func=ACT.Square, accum_out=sy[:])
+            else:
+                nc.vector.scalar_tensor_tensor(out=j2[:], in0=t[:], scalar=0.0, in1=t[:],
+                                               op0=ALU.max, op1=ALU.mult, accum_out=sy[:])
+
+        def op_gb(i):
+            syc = small.tile([P, 1], F32, name="syc", tag="syc")
+            mr = small.tile([P, 2], F32, name="mr", tag="mr")
+            st[("mr", i)] = mr
+            nc.gpsimd.tensor_scalar(out=syc[:], in0=st[("sy", i)][:], scalar1=BIG, scalar2=SS_LO,
+                                    op0=ALU.min, op1=ALU.max)
+            nc.gpsimd.tensor_tensor(out=mr[:], in0=syc[:, 0:1].to_broadcast([P, 2]), in1=expo[:], op=ALU.pow)
+
+        def op_th(i):
+            th = small.tile([P, 1], F32, name="th", tag="th")
+            st[("th", i)] = th
+            nc.scalar.activation(out=th[:], in_=st[("mr", i)][:, 0:1], func=ACT.Tanh)
+
+        def op_gm(i):
+            gg = small.tile([P, 1], F32, name="gg", tag="gg")
+            st[("gg", i)] = gg
+            nc.gpsimd.tensor_tensor(out=gg[:], in0=st[("th", i)][:], in1=st[("mr", i)][:, 1:2], op=ALU.mult)
+
+        def op_pc(i):
+            t = st[("t", i)]
+            gg = st[("gg", i)]
+            if i in P3_V:
+                nc.vector.tensor_scalar(out=t[:], in0=t[:], scalar1=0.0, scalar2=gg[:, 0:1],
+                                        op0=ALU.max, op1=ALU.mult)
+            else:
+                nc.scalar.activation(out=t[:], in_=t[:], func=ACT.Relu, scale=gg[:, 0:1])
+
+        def op_st(i):
+            nc.sync.dma_start(out=out[i * P:(i + 1) * P, :], in_=st[("t", i)][:])
+
+        table = {
+            "v_ms": op_v_ms, "g_id": op_g_id, "s_dummy": op_s_dummy, "ld_b": op_ld_b,
+            "ld_mid": op_ld_mid, "ld_w": op_ld_w, "pe_b": op_pe_b, "bcp": op_bcp, "sq": op_sq,
+            "ga": op_ga, "ln": op_ln, "f": op_f, "d": op_d, "tr": op_tr, "cp": op_cp, "uq": op_uq,
+            "wr": op_wr, "wq": op_wq, "mx": op_mx, "pa": op_pa, "rl": op_rl, "pb": op_pb,
+            "gb": op_gb, "th": op_th, "gm": op_gm, "pc": op_pc, "st": op_st,
+        }
+        for kind, idx in ORDER:
+            table[kind](idx)

@@ -18,13 +18,12 @@ HALF = 512
 EPS = 1e-7
 SS_LO = EPS * EPS
 SS_HI = (1.0 - EPS) * (1.0 - EPS)
-BIG = 3.0e38
+NB = 4
 
-ORDER = [["v_ms",0],["g_id",0],["ld_mid",0],["s_dummy",0],["ld_b",0],["ld_w",0],["ld_mid",1],["pe_b",0],["ld_w",1],["sq",0],["bcp",0],["ld_mid",2],["wr",0],["ga",0],["ld_w",2],["sq",1],["ld_mid",3],["wr",1],["ln",0],["ga",1],["ld_w",3],["sq",2],["wq",0],["ld_mid",4],["f",0],["wr",2],["ga",2],["ld_mid",5],["sq",3],["ld_mid",6],["wq",2],["ld_mid",7],["ln",1],["ln",2],["ga",3],["bcp",1],["sq",4],["d",0],["wr",3],["tr",0],["ln",3],["sq",6],["ga",4],["f",1],["f",3],["wq",1],["sq",5],["f",2],["ga",6],["d",3],["d",2],["wq",3],["tr",2],["ln",4],["cp",0],["ga",5],["f",4],["d",1],["d",4],["tr",1],["ln",6],["uq",0],["ln",5],["cp",1],["f",5],["f",6],["d",5],["mx",0],["d",6],["cp",2],["uq",1],["tr",3],["pa",0],["mx",1],["sq",7],["uq",2],["pb",0],["cp",3],["mx",2],["ga",7],["pa",1],["tr",4],["gb",0],["ln",7],["tr",5],["f",7],["pa",2],["tr",6],["cp",5],["uq",3],["cp",6],["d",7],["pb",1],["tr",7],["cp",4],["mx",3],["pb",2],["gb",1],["th",0],["uq",4],["gb",2],["uq",5],["uq",6],["mx",4],["pa",3],["cp",7],["gm",0],["pa",4],["mx",5],["pc",0],["pb",3],["mx",6],["th",2],["th",1],["st",0],["gm",2],["gm",1],["uq",7],["gb",3],["pa",5],["th",3],["gm",3],["pb",5],["mx",7],["pc",3],["pb",4],["gb",5],["pc",1],["pa",6],["gb",4],["th",5],["pc",2],["st",1],["gm",5],["pb",6],["th",4],["st",2],["gm",4],["pc",4],["pa",7],["gb",6],["st",3],["th",6],["pc",5],["pb",7],["st",4],["gm",6],["pc",6],["st",5],["gb",7],["th",7],["st",6],["gm",7],["pc",7],["st",7]]
+ORDER = [["v_ms",0],["g_id",0],["ld_mid",0],["s_dummy",0],["ld_b",0],["ld_w",0],["ld_mid",1],["pe_b",0],["ld_mid",2],["sq",0],["ld_w",1],["bcp",1],["wr",0],["ld_mid",3],["sq",1],["ld_w",2],["wq",0],["sq",2],["ld_mid",4],["wr",1],["ld_w",3],["sq",3],["wq",1],["ld_mid",5],["bcp",0],["gc",0],["ld_mid",6],["gp",0],["sq",4],["ld_mid",7],["rc",0],["ln",1],["wr",2],["ln",0],["ln",3],["ln",2],["sq",5],["f",0],["d",0],["sq",6],["wq",2],["tr",0],["d",1],["cp",0],["d",2],["tr",1],["wr",3],["tr",2],["cp",1],["wq",3],["uq",0],["sq",7],["d",3],["mx",0],["uq",1],["cp",2],["gc",1],["gp",1],["mx",1],["pa",0],["ln",7],["ln",4],["ln",6],["ln",5],["pb",0],["tr",3],["cp",3],["rc",1],["uq",2],["f",1],["pa",1],["gb",0],["mx",2],["th",0],["d",6],["d",4],["tr",6],["pb",1],["tr",4],["cp",6],["uq",3],["pa",2],["gb",1],["mx",3],["cp",4],["d",5],["pb",2],["tr",5],["cp",5],["uq",4],["pa",3],["gb",2],["mx",4],["pc",0],["uq",6],["d",7],["th",1],["uq",5],["st",0],["tr",7],["pb",3],["mx",5],["cp",7],["pa",4],["gb",3],["th",2],["pc",2],["pb",4],["mx",6],["pc",1],["uq",7],["pa",5],["gb",4],["th",3],["st",1],["th",4],["pb",5],["pc",4],["mx",7],["st",2],["pc",3],["pa",6],["gb",5],["th",5],["st",3],["pb",6],["pc",5],["st",4],["pa",7],["gb",6],["st",5],["th",6],["pb",7],["pc",6],["st",6],["gb",7],["th",7],["pc",7],["st",7]]
 PINNED = True
 CP_V = []
-P2_S = []
-P3_V = []
+P3_V = [7]
 
 
 def tile_graphconvhyp_pb_kernel(tc, mid, W, b, out):
@@ -49,8 +48,9 @@ def tile_graphconvhyp_pb_kernel(tc, mid, W, b, out):
         brow = const.tile([P, 1024], BF16, name="brow")
         b_bc = const.tile([P, 1024], BF16, name="b_bc")
         expo = const.tile([P, 2], F32, name="expo")
+        halfs = const.tile([P, NB], F32, name="halfs")
         sgn = const.tile([P, 2], F32, name="sgn")
-        dm_in = const.tile([P, 1], F32, name="dm_in")
+        onec = const.tile([P, 1], F32, name="onec")
         dm_out = const.tile([P, 1], F32, name="dm_out")
         wcodes = const.tile([P, 2, 1024], U32, name="wcodes", align_bytes=64)
         wscales = const.tile([P, 2, 1024], U8, name="wscales", align_bytes=64)
@@ -59,12 +59,19 @@ def tile_graphconvhyp_pb_kernel(tc, mid, W, b, out):
 
         st = {}
 
+        def batch_tile(kind, bi, shape):
+            key = (kind, bi)
+            if key not in st:
+                st[key] = small.tile(shape, F32, name=kind, tag=kind)
+            return st[key]
+
         def op_v_ms(i):
-            nc.vector.memset(dm_in[:], 1.0)
+            nc.vector.memset(onec[:], 1.0)
             nc.vector.memset(brow[:], 0.0)
             nc.vector.memset(ones[:], 1.0)
 
         def op_g_id(i):
+            nc.gpsimd.memset(halfs[:], 0.5)
             nc.gpsimd.memset(expo[:, 0:1], 0.5)
             nc.gpsimd.memset(expo[:, 1:2], -0.5)
             nc.gpsimd.memset(sgn[:, 0:1], 1.0)
@@ -72,7 +79,7 @@ def tile_graphconvhyp_pb_kernel(tc, mid, W, b, out):
             make_identity(nc, ident[:])
 
         def op_s_dummy(i):
-            nc.scalar.activation(out=dm_out[:], in_=dm_in[:], func=ACT.Ln)
+            nc.scalar.activation(out=dm_out[:], in_=onec[:], func=ACT.Ln)
 
         def op_ld_b(i):
             nc.scalar.dma_start(out=brow[0:1, :], in_=b.rearrange("(o n) -> o n", o=1))
@@ -106,39 +113,43 @@ def tile_graphconvhyp_pb_kernel(tc, mid, W, b, out):
             nc.vector.tensor_copy(out=b_bc[:, nh * HALF:(nh + 1) * HALF], in_=st[("pbias", nh)][:])
 
         def op_sq(i):
+            bi, k = divmod(i, NB)
             sj = junk.tile([P, 1024], BF16, name="sj", tag="sj")
-            ss = small.tile([P, 1], F32, name="ss", tag="ss")
-            st[("ss", i)] = ss
-            nc.scalar.activation(out=sj[:], in_=st[("mt", i)][:], func=ACT.Square, accum_out=ss[:])
+            ss = batch_tile("ss", bi, [P, NB])
+            nc.scalar.activation(out=sj[:], in_=st[("mt", i)][:], func=ACT.Square,
+                                 accum_out=ss[:, k:k + 1])
 
-        def op_ga(i):
-            ssc = small.tile([P, 1], F32, name="ssc", tag="ssc")
-            nr = small.tile([P, 2], F32, name="nr", tag="nr")
-            pm = small.tile([P, 2], F32, name="pm", tag="pm")
-            st[("nr", i)] = nr
-            st[("pm", i)] = pm
-            nc.gpsimd.tensor_scalar(out=ssc[:], in0=st[("ss", i)][:], scalar1=SS_HI, scalar2=SS_LO,
+        def op_gc(bi):
+            ssc = batch_tile("ssc", bi, [P, NB])
+            nc.gpsimd.tensor_scalar(out=ssc[:], in0=st[("ss", bi)][:], scalar1=SS_HI, scalar2=SS_LO,
                                     op0=ALU.min, op1=ALU.max)
-            nc.gpsimd.tensor_tensor(out=nr[:], in0=ssc[:, 0:1].to_broadcast([P, 2]), in1=expo[:], op=ALU.pow)
-            nc.gpsimd.tensor_scalar(out=pm[:], in0=sgn[:], scalar1=nr[:, 0:1], scalar2=1.0,
-                                    op0=ALU.mult, op1=ALU.add)
+
+        def op_gp(bi):
+            nn = batch_tile("nn", bi, [P, NB])
+            nc.gpsimd.tensor_tensor(out=nn[:], in0=st[("ssc", bi)][:], in1=halfs[:], op=ALU.pow)
+
+        def op_rc(bi):
+            rn = batch_tile("rn", bi, [P, NB])
+            nc.vector.reciprocal(out=rn[:], in_=st[("nn", bi)][:])
 
         def op_ln(i):
-            lg = small.tile([P, 2], F32, name="lg", tag="lg")
-            st[("lg", i)] = lg
-            nc.scalar.activation(out=lg[:], in_=st[("pm", i)][:], func=ACT.Ln)
+            bi, k = divmod(i, NB)
+            lg = batch_tile("lg", bi, [P, NB, 2])
+            nc.scalar.activation(out=lg[:, k, :], in_=sgn[:], func=ACT.Ln,
+                                 scale=st[("nn", bi)][:, k:k + 1], bias=onec[:, 0:1])
 
-        def op_f(i):
-            f2 = small.tile([P, 1], F32, name="f2", tag="f2")
-            st[("f2", i)] = f2
-            lg = st[("lg", i)]
-            nc.vector.scalar_tensor_tensor(out=f2[:], in0=lg[:, 0:1], scalar=lg[:, 1:2],
-                                           in1=st[("nr", i)][:, 1:2], op0=ALU.subtract, op1=ALU.mult)
+        def op_f(bi):
+            lg = st[("lg", bi)]
+            df = batch_tile("df", bi, [P, NB])
+            f2 = batch_tile("f2", bi, [P, NB])
+            nc.vector.tensor_tensor(out=df[:], in0=lg[:, :, 0], in1=lg[:, :, 1], op=ALU.subtract)
+            nc.vector.tensor_tensor(out=f2[:], in0=df[:], in1=st[("rn", bi)][:], op=ALU.mult)
 
         def op_d(i):
+            bi, k = divmod(i, NB)
             u = up.tile([P, 1024], BF16, name="u", tag="u")
             st[("u", i)] = u
-            nc.vector.tensor_scalar(out=u[:], in0=st[("mt", i)][:], scalar1=st[("f2", i)][:, 0:1],
+            nc.vector.tensor_scalar(out=u[:], in0=st[("mt", i)][:], scalar1=st[("f2", bi)][:, k:k + 1],
                                     scalar2=0.5, op0=ALU.mult, op1=ALU.mult)
 
         def op_tr(i):
@@ -204,38 +215,29 @@ def tile_graphconvhyp_pb_kernel(tc, mid, W, b, out):
                 nc.vector.tensor_tensor(out=t[:, nh * HALF:(nh + 1) * HALF], in0=st[("acc", i, nh)][:],
                                         in1=b_bc[:, nh * HALF:(nh + 1) * HALF], op=ALU.add)
 
-        def op_rl(i):
-            t = st[("t", i)]
-            nc.scalar.activation(out=t[:], in_=t[:], func=ACT.Relu)
-
         def op_pb(i):
             t = st[("t", i)]
             j2 = junk.tile([P, 1024], F32, name="j2", tag="j2")
             sy = small.tile([P, 1], F32, name="sy", tag="sy")
-            st[("sy", i)] = sy
-            if i in P2_S:
-                nc.scalar.activation(out=j2[:], in_=t[:], func=ACT.Square, accum_out=sy[:])
-            else:
-                nc.vector.scalar_tensor_tensor(out=j2[:], in0=t[:], scalar=0.0, in1=t[:],
-                                               op0=ALU.max, op1=ALU.mult, accum_out=sy[:])
+            syc = small.tile([P, 1], F32, name="syc", tag="syc")
+            st[("syc", i)] = syc
+            nc.vector.scalar_tensor_tensor(out=j2[:], in0=t[:], scalar=0.0, in1=t[:],
+                                           op0=ALU.max, op1=ALU.mult, accum_out=sy[:])
+            nc.vector.tensor_scalar(out=syc[:], in0=sy[:], scalar1=SS_LO, scalar2=None, op0=ALU.max)
 
         def op_gb(i):
-            syc = small.tile([P, 1], F32, name="syc", tag="syc")
             mr = small.tile([P, 2], F32, name="mr", tag="mr")
             st[("mr", i)] = mr
-            nc.gpsimd.tensor_scalar(out=syc[:], in0=st[("sy", i)][:], scalar1=BIG, scalar2=SS_LO,
-                                    op0=ALU.min, op1=ALU.max)
-            nc.gpsimd.tensor_tensor(out=mr[:], in0=syc[:, 0:1].to_broadcast([P, 2]), in1=expo[:], op=ALU.pow)
+            nc.gpsimd.tensor_tensor(out=mr[:], in0=st[("syc", i)][:, 0:1].to_broadcast([P, 2]),
+                                    in1=expo[:], op=ALU.pow)
 
         def op_th(i):
             th = small.tile([P, 1], F32, name="th", tag="th")
-            st[("th", i)] = th
-            nc.scalar.activation(out=th[:], in_=st[("mr", i)][:, 0:1], func=ACT.Tanh)
-
-        def op_gm(i):
             gg = small.tile([P, 1], F32, name="gg", tag="gg")
             st[("gg", i)] = gg
-            nc.gpsimd.tensor_tensor(out=gg[:], in0=st[("th", i)][:], in1=st[("mr", i)][:, 1:2], op=ALU.mult)
+            mr = st[("mr", i)]
+            nc.scalar.activation(out=th[:], in_=mr[:, 0:1], func=ACT.Tanh)
+            nc.scalar.activation(out=gg[:], in_=th[:], func=ACT.Copy, scale=mr[:, 1:2])
 
         def op_pc(i):
             t = st[("t", i)]
@@ -252,9 +254,9 @@ def tile_graphconvhyp_pb_kernel(tc, mid, W, b, out):
         table = {
             "v_ms": op_v_ms, "g_id": op_g_id, "s_dummy": op_s_dummy, "ld_b": op_ld_b,
             "ld_mid": op_ld_mid, "ld_w": op_ld_w, "pe_b": op_pe_b, "bcp": op_bcp, "sq": op_sq,
-            "ga": op_ga, "ln": op_ln, "f": op_f, "d": op_d, "tr": op_tr, "cp": op_cp, "uq": op_uq,
-            "wr": op_wr, "wq": op_wq, "mx": op_mx, "pa": op_pa, "rl": op_rl, "pb": op_pb,
-            "gb": op_gb, "th": op_th, "gm": op_gm, "pc": op_pc, "st": op_st,
+            "gc": op_gc, "gp": op_gp, "rc": op_rc, "ln": op_ln, "f": op_f, "d": op_d, "tr": op_tr,
+            "cp": op_cp, "uq": op_uq, "wr": op_wr, "wq": op_wq, "mx": op_mx, "pa": op_pa,
+            "pb": op_pb, "gb": op_gb, "th": op_th, "pc": op_pc, "st": op_st,
         }
         for kind, idx in ORDER:
             table[kind](idx)

@@ -14,249 +14,272 @@ ALU = mybir.AluOpType
 ACT = mybir.ActivationFunctionType
 
 P = 128
-HALF = 512
+SIZE = 1024
+ROW_TILES = SIZE // P
+PACK = 4
+K_PASS = P * PACK
+PASSES = SIZE // K_PASS
+BANK = 512
+HALVES = SIZE // BANK
+BATCH = 4
 EPS = 1e-7
-SS_LO = EPS * EPS
-SS_HI = (1.0 - EPS) * (1.0 - EPS)
-NB = 4
-
-ORDER = [["v_ms",0],["g_id",0],["ld_mid",0],["s_dummy",0],["ld_b",0],["ld_w",0],["ld_mid",1],["pe_b",0],["ld_mid",2],["sq",0],["ld_w",1],["bcp",1],["wr",0],["ld_mid",3],["sq",1],["ld_w",2],["wq",0],["sq",2],["ld_mid",4],["wr",1],["ld_w",3],["sq",3],["wq",1],["ld_mid",5],["bcp",0],["gc",0],["ld_mid",6],["gp",0],["sq",4],["ld_mid",7],["rc",0],["ln",1],["wr",2],["ln",0],["ln",3],["ln",2],["sq",5],["f",0],["d",0],["sq",6],["wq",2],["tr",0],["d",1],["cp",0],["d",2],["tr",1],["wr",3],["tr",2],["cp",1],["wq",3],["uq",0],["sq",7],["d",3],["mx",0],["uq",1],["cp",2],["gc",1],["gp",1],["mx",1],["pa",0],["ln",7],["ln",4],["ln",6],["ln",5],["pb",0],["tr",3],["cp",3],["rc",1],["uq",2],["f",1],["pa",1],["gb",0],["mx",2],["th",0],["d",6],["d",4],["tr",6],["pb",1],["tr",4],["cp",6],["uq",3],["pa",2],["gb",1],["mx",3],["cp",4],["d",5],["pb",2],["tr",5],["cp",5],["uq",4],["pa",3],["gb",2],["mx",4],["pc",0],["uq",6],["d",7],["th",1],["uq",5],["st",0],["tr",7],["pb",3],["mx",5],["cp",7],["pa",4],["gb",3],["th",2],["pc",2],["pb",4],["mx",6],["pc",1],["uq",7],["pa",5],["gb",4],["th",3],["st",1],["th",4],["pb",5],["pc",4],["mx",7],["st",2],["pc",3],["pa",6],["gb",5],["th",5],["st",3],["pb",6],["pc",5],["st",4],["pa",7],["gb",6],["st",5],["th",6],["pb",7],["pc",6],["st",6],["gb",7],["th",7],["pc",7],["st",7]]
-PINNED = True
-CP_V = []
-P3_V = [7]
+PIECES = [(0, 0), (1, 0), (0, 1), (1, 1)]
 
 
 def tile_graphconvhyp_pb_kernel(tc, mid, W, b, out):
     nc = tc.nc
     with ExitStack() as ctx:
         const = ctx.enter_context(tc.tile_pool(name="const", bufs=1))
-        midp = ctx.enter_context(tc.tile_pool(name="midp", bufs=8))
-        wrawp = ctx.enter_context(tc.tile_pool(name="wrawp", bufs=4))
-        wgrpp = ctx.enter_context(tc.tile_pool(name="wgrpp", bufs=4))
-        up = ctx.enter_context(tc.tile_pool(name="up", bufs=8))
-        ugp = ctx.enter_context(tc.tile_pool(name="ugp", bufs=8))
-        junk = ctx.enter_context(tc.tile_pool(name="junk", bufs=2))
-        tp = ctx.enter_context(tc.tile_pool(name="tp", bufs=8))
-        small = ctx.enter_context(tc.tile_pool(name="small", bufs=8))
-        pst = ctx.enter_context(tc.psum_pool(name="pst", bufs=4))
-        psa = ctx.enter_context(tc.psum_pool(name="psa", bufs=4))
-        if PINNED:
-            ctx.enter_context(tc.manual_schedule())
+        rows_in = ctx.enter_context(tc.tile_pool(name="rows_in", bufs=ROW_TILES))
+        w_in = ctx.enter_context(tc.tile_pool(name="w_in", bufs=len(PIECES)))
+        w_grouped = ctx.enter_context(tc.tile_pool(name="w_grouped", bufs=len(PIECES)))
+        u_rows = ctx.enter_context(tc.tile_pool(name="u_rows", bufs=ROW_TILES))
+        u_grouped = ctx.enter_context(tc.tile_pool(name="u_grouped", bufs=ROW_TILES))
+        unread = ctx.enter_context(tc.tile_pool(name="unread", bufs=2))
+        y_rows = ctx.enter_context(tc.tile_pool(name="y_rows", bufs=ROW_TILES))
+        stats = ctx.enter_context(tc.tile_pool(name="stats", bufs=ROW_TILES))
+        ps_t = ctx.enter_context(tc.psum_pool(name="ps_t", bufs=4))
+        ps_y = ctx.enter_context(tc.psum_pool(name="ps_y", bufs=4))
+        ctx.enter_context(tc.manual_schedule())
 
         ident = const.tile([P, P], BF16, name="ident")
         ones = const.tile([P, P], BF16, name="ones")
-        brow = const.tile([P, 1024], BF16, name="brow")
-        b_bc = const.tile([P, 1024], BF16, name="b_bc")
-        expo = const.tile([P, 2], F32, name="expo")
-        halfs = const.tile([P, NB], F32, name="halfs")
-        sgn = const.tile([P, 2], F32, name="sgn")
-        onec = const.tile([P, 1], F32, name="onec")
-        dm_out = const.tile([P, 1], F32, name="dm_out")
-        wcodes = const.tile([P, 2, 1024], U32, name="wcodes", align_bytes=64)
-        wscales = const.tile([P, 2, 1024], U8, name="wscales", align_bytes=64)
-        ucodes = const.tile([P, 8, 256], U32, name="ucodes", align_bytes=64)
-        uscales = const.tile([P, 8, 256], U8, name="uscales", align_bytes=64)
+        b_row = const.tile([P, SIZE], BF16, name="b_row")
+        b_all = const.tile([P, SIZE], BF16, name="b_all")
+        one = const.tile([P, 1], F32, name="one")
+        warm = const.tile([P, 1], F32, name="warm")
+        plus_minus = const.tile([P, 2], F32, name="plus_minus")
+        half = const.tile([P, BATCH], F32, name="half")
+        half_pm = const.tile([P, 2], F32, name="half_pm")
+        w_codes = const.tile([P, PASSES, SIZE], U32, name="w_codes", align_bytes=64)
+        w_scales = const.tile([P, PASSES, SIZE], U8, name="w_scales", align_bytes=64)
+        u_codes = const.tile([P, ROW_TILES, PASSES * P], U32, name="u_codes", align_bytes=64)
+        u_scales = const.tile([P, ROW_TILES, PASSES * P], U8, name="u_scales", align_bytes=64)
 
-        st = {}
+        mid_t = {}
+        w_raw = {}
+        w_grp = {}
+        n_sq, n_clip, norm, inv_norm, logs, factor = {}, {}, {}, {}, {}, {}
+        u_t, u_ps, u_grp = {}, {}, {}
+        b_ps, y_ps = {}, {}
+        y_t, m_sq, m_both, gain = {}, {}, {}, {}
 
-        def batch_tile(kind, bi, shape):
-            key = (kind, bi)
-            if key not in st:
-                st[key] = small.tile(shape, F32, name=kind, tag=kind)
-            return st[key]
+        def load_rows(i):
+            mid_t[i] = rows_in.tile([P, SIZE], BF16, name="mid_t")
+            nc.sync.dma_start(out=mid_t[i][:], in_=mid[i * P:(i + 1) * P, :])
 
-        def op_v_ms(i):
-            nc.vector.memset(onec[:], 1.0)
-            nc.vector.memset(brow[:], 0.0)
-            nc.vector.memset(ones[:], 1.0)
-
-        def op_g_id(i):
-            nc.gpsimd.memset(halfs[:], 0.5)
-            nc.gpsimd.memset(expo[:, 0:1], 0.5)
-            nc.gpsimd.memset(expo[:, 1:2], -0.5)
-            nc.gpsimd.memset(sgn[:, 0:1], 1.0)
-            nc.gpsimd.memset(sgn[:, 1:2], -1.0)
-            make_identity(nc, ident[:])
-
-        def op_s_dummy(i):
-            nc.scalar.activation(out=dm_out[:], in_=onec[:], func=ACT.Ln)
-
-        def op_ld_b(i):
-            nc.scalar.dma_start(out=brow[0:1, :], in_=b.rearrange("(o n) -> o n", o=1))
-
-        def op_ld_mid(i):
-            mt = midp.tile([P, 1024], BF16, name="mt", tag="mt")
-            st[("mt", i)] = mt
-            nc.sync.dma_start(out=mt[:], in_=mid[i * P:(i + 1) * P, :])
-
-        def op_ld_w(j):
-            g, nh = divmod(j, 2)
-            wr = wrawp.tile([P, 4, HALF], BF16, name="wr", tag="wr")
-            st[("wr", j)] = wr
+        def load_w(q):
+            g, h = PIECES[q]
+            w_raw[q] = w_in.tile([P, PACK, BANK], BF16, name="w_raw")
             nc.sync.dma_start(
-                out=wr[:],
-                in_=W[g * 512:(g + 1) * 512, nh * HALF:(nh + 1) * HALF].rearrange(
-                    "(t p) n -> p t n", t=4, p=P
+                out=w_raw[q][:],
+                in_=W[g * K_PASS:(g + 1) * K_PASS, h * BANK:(h + 1) * BANK].rearrange(
+                    "(t p) n -> p t n", t=PACK, p=P
                 ),
             )
 
-        def op_pe_b(i):
-            for nh in range(2):
-                pb = psa.tile([P, HALF], F32, name="pb", tag="acc")
-                st[("pbias", nh)] = pb
-                nc.tensor.matmul(
-                    out=pb[:], lhsT=ones[:], rhs=brow[:, nh * HALF:(nh + 1) * HALF],
-                    start=True, stop=True,
-                )
-
-        def op_bcp(nh):
-            nc.vector.tensor_copy(out=b_bc[:, nh * HALF:(nh + 1) * HALF], in_=st[("pbias", nh)][:])
-
-        def op_sq(i):
-            bi, k = divmod(i, NB)
-            sj = junk.tile([P, 1024], BF16, name="sj", tag="sj")
-            ss = batch_tile("ss", bi, [P, NB])
-            nc.scalar.activation(out=sj[:], in_=st[("mt", i)][:], func=ACT.Square,
-                                 accum_out=ss[:, k:k + 1])
-
-        def op_gc(bi):
-            ssc = batch_tile("ssc", bi, [P, NB])
-            nc.gpsimd.tensor_scalar(out=ssc[:], in0=st[("ss", bi)][:], scalar1=SS_HI, scalar2=SS_LO,
-                                    op0=ALU.min, op1=ALU.max)
-
-        def op_gp(bi):
-            nn = batch_tile("nn", bi, [P, NB])
-            nc.gpsimd.tensor_tensor(out=nn[:], in0=st[("ssc", bi)][:], in1=halfs[:], op=ALU.pow)
-
-        def op_rc(bi):
-            rn = batch_tile("rn", bi, [P, NB])
-            nc.vector.reciprocal(out=rn[:], in_=st[("nn", bi)][:])
-
-        def op_ln(i):
-            bi, k = divmod(i, NB)
-            lg = batch_tile("lg", bi, [P, NB, 2])
-            nc.scalar.activation(out=lg[:, k, :], in_=sgn[:], func=ACT.Ln,
-                                 scale=st[("nn", bi)][:, k:k + 1], bias=onec[:, 0:1])
-
-        def op_f(bi):
-            lg = st[("lg", bi)]
-            df = batch_tile("df", bi, [P, NB])
-            f2 = batch_tile("f2", bi, [P, NB])
-            nc.vector.tensor_tensor(out=df[:], in0=lg[:, :, 0], in1=lg[:, :, 1], op=ALU.subtract)
-            nc.vector.tensor_tensor(out=f2[:], in0=df[:], in1=st[("rn", bi)][:], op=ALU.mult)
-
-        def op_d(i):
-            bi, k = divmod(i, NB)
-            u = up.tile([P, 1024], BF16, name="u", tag="u")
-            st[("u", i)] = u
-            nc.vector.tensor_scalar(out=u[:], in0=st[("mt", i)][:], scalar1=st[("f2", bi)][:, k:k + 1],
-                                    scalar2=0.5, op0=ALU.mult, op1=ALU.mult)
-
-        def op_tr(i):
-            xt = pst.tile([P, 2, 4, P], BF16, name="xt", tag="xt")
-            st[("xt", i)] = xt
-            u = st[("u", i)]
-            for g in range(2):
-                for t in range(4):
-                    c0 = (g * 4 + t) * P
-                    nc.tensor.transpose(xt[:, g, t, :], u[:, c0:c0 + P], ident[:])
-
-        def op_cp(i):
-            ug = ugp.tile([P, 2, P, 4], BF16, name="ug", tag="ug", align_bytes=64)
-            st[("ug", i)] = ug
-            src = st[("xt", i)][:].rearrange("p g t r -> p g r t")
-            if i in CP_V:
-                nc.vector.tensor_copy(out=ug[:], in_=src)
-            else:
-                nc.scalar.copy(out=ug[:], in_=src)
-
-        def op_uq(i):
-            nc.vector.quantize_mx(
-                out=ucodes[:, i, :].bitcast(FP8X4),
-                scales=uscales[:, i, :],
-                in_=st[("ug", i)][:].rearrange("p g r t -> p (g r t)"),
-            )
-
-        def op_wr(j):
-            wg = wgrpp.tile([P, HALF, 4], BF16, name="wg", tag="wg", align_bytes=64)
-            st[("wg", j)] = wg
+        def regroup_w(q):
+            w_grp[q] = w_grouped.tile([P, BANK, PACK], BF16, name="w_grp", align_bytes=64)
             nc.vector.tensor_copy(
-                out=wg[:].rearrange("p (c i) t -> p c t i", i=4),
-                in_=st[("wr", j)][:].rearrange("p t (c i) -> p c t i", i=4),
+                out=w_grp[q][:].rearrange("p (c i) t -> p c t i", i=4),
+                in_=w_raw[q][:].rearrange("p t (c i) -> p c t i", i=4),
             )
 
-        def op_wq(j):
-            g, nh = divmod(j, 2)
+        def quantise_w(q):
+            g, h = PIECES[q]
             nc.vector.quantize_mx(
-                out=wcodes[:, g, nh * HALF:(nh + 1) * HALF].bitcast(FP8X4),
-                scales=wscales[:, g, nh * HALF:(nh + 1) * HALF],
-                in_=st[("wg", j)][:].rearrange("p n t -> p (n t)"),
+                out=w_codes[:, g, h * BANK:(h + 1) * BANK].bitcast(FP8X4),
+                scales=w_scales[:, g, h * BANK:(h + 1) * BANK],
+                in_=w_grp[q][:].rearrange("p n t -> p (n t)"),
             )
 
-        def op_mx(i):
-            for nh in range(2):
-                acc = psa.tile([P, HALF], F32, name="acc", tag="acc")
-                st[("acc", i, nh)] = acc
-                for g in range(2):
+        def square_sum(i):
+            bt, c = divmod(i, BATCH)
+            if c == 0:
+                n_sq[bt] = stats.tile([P, BATCH], F32, name="n_sq")
+            squares = unread.tile([P, SIZE], BF16, name="squares")
+            nc.scalar.activation(out=squares[:], in_=mid_t[i][:], func=ACT.Square,
+                                 accum_out=n_sq[bt][:, c:c + 1])
+
+        def norm_root(bt):
+            n_clip[bt] = stats.tile([P, BATCH], F32, name="n_clip")
+            norm[bt] = stats.tile([P, BATCH], F32, name="norm")
+            nc.gpsimd.tensor_scalar(out=n_clip[bt][:], in0=n_sq[bt][:],
+                                    scalar1=(1.0 - EPS) * (1.0 - EPS), scalar2=EPS * EPS,
+                                    op0=ALU.min, op1=ALU.max)
+            nc.gpsimd.tensor_tensor(out=norm[bt][:], in0=n_clip[bt][:], in1=half[:], op=ALU.pow)
+
+        def norm_recip(bt):
+            inv_norm[bt] = stats.tile([P, BATCH], F32, name="inv_norm")
+            nc.vector.reciprocal(out=inv_norm[bt][:], in_=norm[bt][:])
+
+        def log_terms(i):
+            bt, c = divmod(i, BATCH)
+            if c == 0:
+                logs[bt] = stats.tile([P, BATCH, 2], F32, name="logs")
+            nc.scalar.activation(out=logs[bt][:, c, :], in_=plus_minus[:], func=ACT.Ln,
+                                 scale=norm[bt][:, c:c + 1], bias=one[:, 0:1])
+
+        def scale_factor(bt):
+            diff = stats.tile([P, BATCH], F32, name="diff")
+            factor[bt] = stats.tile([P, BATCH], F32, name="factor")
+            nc.vector.tensor_tensor(out=diff[:], in0=logs[bt][:, :, 0], in1=logs[bt][:, :, 1],
+                                    op=ALU.subtract)
+            nc.vector.tensor_tensor(out=factor[bt][:], in0=diff[:], in1=inv_norm[bt][:],
+                                    op=ALU.mult)
+
+        def scale_rows(i):
+            bt, c = divmod(i, BATCH)
+            u_t[i] = u_rows.tile([P, SIZE], BF16, name="u_t")
+            nc.vector.tensor_scalar(out=u_t[i][:], in0=mid_t[i][:],
+                                    scalar1=factor[bt][:, c:c + 1], scalar2=0.5,
+                                    op0=ALU.mult, op1=ALU.mult)
+
+        def transpose_rows(i):
+            u_ps[i] = ps_t.tile([P, PASSES, PACK, P], BF16, name="u_ps")
+            for g in range(PASSES):
+                for t in range(PACK):
+                    first = g * K_PASS + t * P
+                    nc.tensor.transpose(u_ps[i][:, g, t, :], u_t[i][:, first:first + P], ident[:])
+
+        def regroup_rows(i):
+            u_grp[i] = u_grouped.tile([P, PASSES, P, PACK], BF16, name="u_grp", align_bytes=64)
+            nc.scalar.copy(out=u_grp[i][:], in_=u_ps[i][:].rearrange("p g t r -> p g r t"))
+
+        def quantise_rows(i):
+            nc.vector.quantize_mx(
+                out=u_codes[:, i, :].bitcast(FP8X4),
+                scales=u_scales[:, i, :],
+                in_=u_grp[i][:].rearrange("p g r t -> p (g r t)"),
+            )
+
+        def multiply(i):
+            for h in range(HALVES):
+                y_ps[i, h] = ps_y.tile([P, BANK], F32, name="y_ps", tag="y_ps")
+                for g in range(PASSES):
                     nc.tensor.matmul_mx(
-                        out=acc[:],
-                        lhsT=ucodes[:, i, g * P:(g + 1) * P].bitcast(FP8X4),
-                        lhsT_scale=uscales[:, i, g * P:(g + 1) * P],
-                        rhs=wcodes[:, g, nh * HALF:(nh + 1) * HALF].bitcast(FP8X4),
-                        rhs_scale=wscales[:, g, nh * HALF:(nh + 1) * HALF],
+                        out=y_ps[i, h][:],
+                        lhsT=u_codes[:, i, g * P:(g + 1) * P].bitcast(FP8X4),
+                        lhsT_scale=u_scales[:, i, g * P:(g + 1) * P],
+                        rhs=w_codes[:, g, h * BANK:(h + 1) * BANK].bitcast(FP8X4),
+                        rhs_scale=w_scales[:, g, h * BANK:(h + 1) * BANK],
                         start=(g == 0),
-                        stop=(g == 1),
+                        stop=(g == PASSES - 1),
                     )
 
-        def op_pa(i):
-            t = tp.tile([P, 1024], F32, name="t", tag="t")
-            st[("t", i)] = t
-            for nh in range(2):
-                nc.vector.tensor_tensor(out=t[:, nh * HALF:(nh + 1) * HALF], in0=st[("acc", i, nh)][:],
-                                        in1=b_bc[:, nh * HALF:(nh + 1) * HALF], op=ALU.add)
+        def add_bias(i):
+            y_t[i] = y_rows.tile([P, SIZE], F32, name="y_t")
+            for h in range(HALVES):
+                nc.vector.tensor_tensor(out=y_t[i][:, h * BANK:(h + 1) * BANK], in0=y_ps[i, h][:],
+                                        in1=b_all[:, h * BANK:(h + 1) * BANK], op=ALU.add)
 
-        def op_pb(i):
-            t = st[("t", i)]
-            j2 = junk.tile([P, 1024], F32, name="j2", tag="j2")
-            sy = small.tile([P, 1], F32, name="sy", tag="sy")
-            syc = small.tile([P, 1], F32, name="syc", tag="syc")
-            st[("syc", i)] = syc
-            nc.vector.scalar_tensor_tensor(out=j2[:], in0=t[:], scalar=0.0, in1=t[:],
-                                           op0=ALU.max, op1=ALU.mult, accum_out=sy[:])
-            nc.vector.tensor_scalar(out=syc[:], in0=sy[:], scalar1=SS_LO, scalar2=None, op0=ALU.max)
+        def sum_squares(i):
+            products = unread.tile([P, SIZE], F32, name="products")
+            total = stats.tile([P, 1], F32, name="total")
+            m_sq[i] = stats.tile([P, 1], F32, name="m_sq")
+            nc.vector.scalar_tensor_tensor(out=products[:], in0=y_t[i][:], scalar=0.0,
+                                           in1=y_t[i][:], op0=ALU.max, op1=ALU.mult,
+                                           accum_out=total[:])
+            nc.vector.tensor_scalar(out=m_sq[i][:], in0=total[:], scalar1=EPS * EPS, scalar2=None,
+                                    op0=ALU.max)
 
-        def op_gb(i):
-            mr = small.tile([P, 2], F32, name="mr", tag="mr")
-            st[("mr", i)] = mr
-            nc.gpsimd.tensor_tensor(out=mr[:], in0=st[("syc", i)][:, 0:1].to_broadcast([P, 2]),
-                                    in1=expo[:], op=ALU.pow)
+        def norm2_root(i):
+            m_both[i] = stats.tile([P, 2], F32, name="m_both")
+            nc.gpsimd.tensor_tensor(out=m_both[i][:], in0=m_sq[i][:, 0:1].to_broadcast([P, 2]),
+                                    in1=half_pm[:], op=ALU.pow)
 
-        def op_th(i):
-            th = small.tile([P, 1], F32, name="th", tag="th")
-            gg = small.tile([P, 1], F32, name="gg", tag="gg")
-            st[("gg", i)] = gg
-            mr = st[("mr", i)]
-            nc.scalar.activation(out=th[:], in_=mr[:, 0:1], func=ACT.Tanh)
-            nc.scalar.activation(out=gg[:], in_=th[:], func=ACT.Copy, scale=mr[:, 1:2])
+        def out_gain(i):
+            tanh_m = stats.tile([P, 1], F32, name="tanh_m")
+            gain[i] = stats.tile([P, 1], F32, name="gain")
+            nc.scalar.activation(out=tanh_m[:], in_=m_both[i][:, 0:1], func=ACT.Tanh)
+            nc.scalar.activation(out=gain[i][:], in_=tanh_m[:], func=ACT.Copy,
+                                 scale=m_both[i][:, 1:2])
 
-        def op_pc(i):
-            t = st[("t", i)]
-            gg = st[("gg", i)]
-            if i in P3_V:
-                nc.vector.tensor_scalar(out=t[:], in0=t[:], scalar1=0.0, scalar2=gg[:, 0:1],
-                                        op0=ALU.max, op1=ALU.mult)
+        def scale_out(i):
+            if i == ROW_TILES - 1:
+                nc.vector.tensor_scalar(out=y_t[i][:], in0=y_t[i][:], scalar1=0.0,
+                                        scalar2=gain[i][:, 0:1], op0=ALU.max, op1=ALU.mult)
             else:
-                nc.scalar.activation(out=t[:], in_=t[:], func=ACT.Relu, scale=gg[:, 0:1])
+                nc.scalar.activation(out=y_t[i][:], in_=y_t[i][:], func=ACT.Relu,
+                                     scale=gain[i][:, 0:1])
+            nc.sync.dma_start(out=out[i * P:(i + 1) * P, :], in_=y_t[i][:])
 
-        def op_st(i):
-            nc.sync.dma_start(out=out[i * P:(i + 1) * P, :], in_=st[("t", i)][:])
+        nc.vector.memset(one[:], 1.0)
+        nc.vector.memset(b_row[:], 0.0)
+        nc.vector.memset(ones[:], 1.0)
+        nc.gpsimd.memset(half[:], 0.5)
+        nc.gpsimd.memset(half_pm[:, 0:1], 0.5)
+        nc.gpsimd.memset(half_pm[:, 1:2], -0.5)
+        nc.gpsimd.memset(plus_minus[:, 0:1], 1.0)
+        nc.gpsimd.memset(plus_minus[:, 1:2], -1.0)
+        make_identity(nc, ident[:])
+        nc.scalar.dma_start(out=b_row[0:1, :], in_=b.rearrange("(o n) -> o n", o=1))
+        nc.scalar.activation(out=warm[:], in_=one[:], func=ACT.Ln)
 
-        table = {
-            "v_ms": op_v_ms, "g_id": op_g_id, "s_dummy": op_s_dummy, "ld_b": op_ld_b,
-            "ld_mid": op_ld_mid, "ld_w": op_ld_w, "pe_b": op_pe_b, "bcp": op_bcp, "sq": op_sq,
-            "gc": op_gc, "gp": op_gp, "rc": op_rc, "ln": op_ln, "f": op_f, "d": op_d, "tr": op_tr,
-            "cp": op_cp, "uq": op_uq, "wr": op_wr, "wq": op_wq, "mx": op_mx, "pa": op_pa,
-            "pb": op_pb, "gb": op_gb, "th": op_th, "pc": op_pc, "st": op_st,
-        }
-        for kind, idx in ORDER:
-            table[kind](idx)
+        load_rows(0)
+        for q in range(len(PIECES)):
+            load_rows(q + 1)
+            load_w(q)
+        for i in range(len(PIECES) + 1, ROW_TILES):
+            load_rows(i)
+
+        for h in range(HALVES):
+            b_ps[h] = ps_y.tile([P, BANK], F32, name="b_ps", tag="y_ps")
+            nc.tensor.matmul(out=b_ps[h][:], lhsT=ones[:], rhs=b_row[:, h * BANK:(h + 1) * BANK],
+                             start=True, stop=True)
+
+        for i in range(BATCH):
+            square_sum(i)
+        regroup_w(0)
+        regroup_w(1)
+        quantise_w(0)
+        norm_root(0)
+        for h in range(HALVES):
+            nc.vector.tensor_copy(out=b_all[:, h * BANK:(h + 1) * BANK], in_=b_ps[h][:])
+        norm_recip(0)
+        square_sum(BATCH)
+        for i in range(BATCH):
+            log_terms(i)
+        for i in range(BATCH + 1, ROW_TILES):
+            square_sum(i)
+        norm_root(1)
+        regroup_w(2)
+        quantise_w(1)
+        scale_factor(0)
+        for i in (0, 1):
+            scale_rows(i)
+            transpose_rows(i)
+        quantise_w(2)
+        regroup_w(3)
+        for i in (2, 3):
+            scale_rows(i)
+            transpose_rows(i)
+        regroup_rows(0)
+        quantise_rows(0)
+        quantise_w(3)
+        regroup_rows(1)
+        quantise_rows(1)
+        regroup_rows(2)
+        for i in range(BATCH, ROW_TILES):
+            log_terms(i)
+        regroup_rows(3)
+        multiply(0)
+        multiply(1)
+
+        for i in range(ROW_TILES):
+            add_bias(i)
+            if i == 1:
+                norm_recip(1)
+                scale_factor(1)
+                for later in range(BATCH, ROW_TILES):
+                    scale_rows(later)
+            if 1 <= i <= BATCH:
+                transpose_rows(i + BATCH - 1)
+                regroup_rows(i + BATCH - 1)
+            sum_squares(i)
+            norm2_root(i)
+            if i + 2 < ROW_TILES:
+                quantise_rows(i + 2)
+                multiply(i + 2)
+            out_gain(i)
+            scale_out(i)

@@ -40,7 +40,6 @@ def tile_graphconvhyp_pb_kernel(tc, mid, W, b, out):
         stats = ctx.enter_context(tc.tile_pool(name="stats", bufs=ROW_TILES))
         ps_t = ctx.enter_context(tc.psum_pool(name="ps_t", bufs=4))
         ps_y = ctx.enter_context(tc.psum_pool(name="ps_y", bufs=4))
-        ctx.enter_context(tc.manual_schedule())
 
         ident = const.tile([P, P], BF16, name="ident")
         ones = const.tile([P, P], BF16, name="ones")

@@ -49,7 +49,7 @@ def tile_graphconvhyp_pb_kernel(tc, mid, W, b, out):
         warm = const.tile([P, 1], F32, name="warm")
         plus_minus = const.tile([P, 2], F32, name="plus_minus")
         half = const.tile([P, BATCH], F32, name="half")
-        half_pm = const.tile([P, 2], F32, name="half_pm")
+        minus_half = const.tile([P, 1], F32, name="minus_half")
         w_codes = const.tile([P, PASSES, SIZE], U32, name="w_codes", align_bytes=64)
         w_scales = const.tile([P, PASSES, SIZE], U8, name="w_scales", align_bytes=64)
         u_codes = const.tile([P, ROW_TILES, PASSES * P], U32, name="u_codes", align_bytes=64)
@@ -61,7 +61,7 @@ def tile_graphconvhyp_pb_kernel(tc, mid, W, b, out):
         n_sq, n_clip, norm, inv_norm, logs, factor = {}, {}, {}, {}, {}, {}
         u_t, u_ps, u_grp = {}, {}, {}
         b_ps, y_ps = {}, {}
-        y_t, m_sq, m_both, gain = {}, {}, {}, {}
+        y_t, m_sq, inv_m, gain = {}, {}, {}, {}
 
         def load_rows(i):
             mid_t[i] = rows_in.tile([P, SIZE], BF16, name="mid_t")
@@ -183,16 +183,14 @@ def tile_graphconvhyp_pb_kernel(tc, mid, W, b, out):
                                     op0=ALU.max)
 
         def norm2_root(i):
-            m_both[i] = stats.tile([P, 2], F32, name="m_both")
-            nc.gpsimd.tensor_tensor(out=m_both[i][:], in0=m_sq[i][:, 0:1].to_broadcast([P, 2]),
-                                    in1=half_pm[:], op=ALU.pow)
+            inv_m[i] = stats.tile([P, 1], F32, name="inv_m")
+            nc.gpsimd.tensor_tensor(out=inv_m[i][:], in0=m_sq[i][:], in1=minus_half[:], op=ALU.pow)
 
         def out_gain(i):
             tanh_m = stats.tile([P, 1], F32, name="tanh_m")
             gain[i] = stats.tile([P, 1], F32, name="gain")
-            nc.scalar.activation(out=tanh_m[:], in_=m_both[i][:, 0:1], func=ACT.Tanh)
-            nc.scalar.activation(out=gain[i][:], in_=tanh_m[:], func=ACT.Copy,
-                                 scale=m_both[i][:, 1:2])
+            nc.scalar.activation(out=tanh_m[:], in_=m_sq[i][:], func=ACT.Tanh, scale=inv_m[i][:, 0:1])
+            nc.scalar.activation(out=gain[i][:], in_=tanh_m[:], func=ACT.Copy, scale=inv_m[i][:, 0:1])
 
         def scale_out(i):
             if i == ROW_TILES - 1:
@@ -207,8 +205,7 @@ def tile_graphconvhyp_pb_kernel(tc, mid, W, b, out):
         nc.vector.memset(b_row[:], 0.0)
         nc.vector.memset(ones[:], 1.0)
         nc.gpsimd.memset(half[:], 0.5)
-        nc.gpsimd.memset(half_pm[:, 0:1], 0.5)
-        nc.gpsimd.memset(half_pm[:, 1:2], -0.5)
+        nc.gpsimd.memset(minus_half[:], -0.5)
         nc.gpsimd.memset(plus_minus[:, 0:1], 1.0)
         nc.gpsimd.memset(plus_minus[:, 1:2], -1.0)
         make_identity(nc, ident[:])
@@ -227,58 +224,29 @@ def tile_graphconvhyp_pb_kernel(tc, mid, W, b, out):
             nc.tensor.matmul(out=b_ps[h][:], lhsT=ones[:], rhs=b_row[:, h * BANK:(h + 1) * BANK],
                              start=True, stop=True)
 
-        for i in range(BATCH):
-            square_sum(i)
-        regroup_w(0)
-        regroup_w(1)
-        quantise_w(0)
-        norm_root(0)
         for h in range(HALVES):
             nc.vector.tensor_copy(out=b_all[:, h * BANK:(h + 1) * BANK], in_=b_ps[h][:])
-        norm_recip(0)
-        square_sum(BATCH)
-        for i in range(BATCH):
-            log_terms(i)
-        for i in range(BATCH + 1, ROW_TILES):
-            square_sum(i)
-        norm_root(1)
-        regroup_w(2)
-        quantise_w(1)
-        scale_factor(0)
-        for i in (0, 1):
-            scale_rows(i)
-            transpose_rows(i)
-        quantise_w(2)
-        regroup_w(3)
-        for i in (2, 3):
-            scale_rows(i)
-            transpose_rows(i)
-        regroup_rows(0)
-        quantise_rows(0)
-        quantise_w(3)
-        regroup_rows(1)
-        quantise_rows(1)
-        regroup_rows(2)
-        for i in range(BATCH, ROW_TILES):
-            log_terms(i)
-        regroup_rows(3)
-        multiply(0)
-        multiply(1)
-
+        for q in range(len(PIECES)):
+            regroup_w(q)
+            quantise_w(q)
+        for bt in range(ROW_TILES // BATCH):
+            tiles = range(bt * BATCH, (bt + 1) * BATCH)
+            for i in tiles:
+                square_sum(i)
+            norm_root(bt)
+            norm_recip(bt)
+            for i in tiles:
+                log_terms(i)
+            scale_factor(bt)
+            for i in tiles:
+                scale_rows(i)
+                transpose_rows(i)
+                regroup_rows(i)
+                quantise_rows(i)
         for i in range(ROW_TILES):
+            multiply(i)
             add_bias(i)
-            if i == 1:
-                norm_recip(1)
-                scale_factor(1)
-                for later in range(BATCH, ROW_TILES):
-                    scale_rows(later)
-            if 1 <= i <= BATCH:
-                transpose_rows(i + BATCH - 1)
-                regroup_rows(i + BATCH - 1)
             sum_squares(i)
             norm2_root(i)
-            if i + 2 < ROW_TILES:
-                quantise_rows(i + 2)
-                multiply(i + 2)
             out_gain(i)
             scale_out(i)

@@ -224,29 +224,58 @@ def tile_graphconvhyp_pb_kernel(tc, mid, W, b, out):
             nc.tensor.matmul(out=b_ps[h][:], lhsT=ones[:], rhs=b_row[:, h * BANK:(h + 1) * BANK],
                              start=True, stop=True)
 
+        for i in range(BATCH):
+            square_sum(i)
+        regroup_w(0)
+        regroup_w(1)
+        quantise_w(0)
+        norm_root(0)
         for h in range(HALVES):
             nc.vector.tensor_copy(out=b_all[:, h * BANK:(h + 1) * BANK], in_=b_ps[h][:])
-        for q in range(len(PIECES)):
-            regroup_w(q)
-            quantise_w(q)
-        for bt in range(ROW_TILES // BATCH):
-            tiles = range(bt * BATCH, (bt + 1) * BATCH)
-            for i in tiles:
-                square_sum(i)
-            norm_root(bt)
-            norm_recip(bt)
-            for i in tiles:
-                log_terms(i)
-            scale_factor(bt)
-            for i in tiles:
-                scale_rows(i)
-                transpose_rows(i)
-                regroup_rows(i)
-                quantise_rows(i)
+        norm_recip(0)
+        square_sum(BATCH)
+        for i in range(BATCH):
+            log_terms(i)
+        for i in range(BATCH + 1, ROW_TILES):
+            square_sum(i)
+        norm_root(1)
+        regroup_w(2)
+        quantise_w(1)
+        scale_factor(0)
+        for i in (0, 1):
+            scale_rows(i)
+            transpose_rows(i)
+        quantise_w(2)
+        regroup_w(3)
+        for i in (2, 3):
+            scale_rows(i)
+            transpose_rows(i)
+        regroup_rows(0)
+        quantise_rows(0)
+        quantise_w(3)
+        regroup_rows(1)
+        quantise_rows(1)
+        regroup_rows(2)
+        for i in range(BATCH, ROW_TILES):
+            log_terms(i)
+        regroup_rows(3)
+        multiply(0)
+        multiply(1)
+
         for i in range(ROW_TILES):
-            multiply(i)
             add_bias(i)
+            if i == 1:
+                norm_recip(1)
+                scale_factor(1)
+                for later in range(BATCH, ROW_TILES):
+                    scale_rows(later)
+            if 1 <= i <= BATCH:
+                transpose_rows(i + BATCH - 1)
+                regroup_rows(i + BATCH - 1)
             sum_squares(i)
             norm2_root(i)
+            if i + 2 < ROW_TILES:
+                quantise_rows(i + 2)
+                multiply(i + 2)
             out_gain(i)
             scale_out(i)

from contextlib import ExitStack

import concourse.mybir as mybir
from concourse.masks import make_identity

FLOPS = 2 * 1024 * 1024 * 1024

F32 = mybir.dt.float32
BF16 = mybir.dt.bfloat16
U32 = mybir.dt.uint32
U8 = mybir.dt.uint8
FP8X4 = mybir.dt.float8_e4m3fn_x4
ALU = mybir.AluOpType
ACT = mybir.ActivationFunctionType

P = 128
SIZE = 1024
ROW_TILES = SIZE // P
PACK = 4
K_PASS = P * PACK
PASSES = SIZE // K_PASS
BANK = 512
HALVES = SIZE // BANK
BATCH = 4
EPS = 1e-7
PIECES = [(0, 0), (1, 0), (0, 1), (1, 1)]


def tile_graphconvhyp_pb_kernel(tc, mid, W, b, out):
    nc = tc.nc
    with ExitStack() as ctx:
        const = ctx.enter_context(tc.tile_pool(name="const", bufs=1))
        rows_in = ctx.enter_context(tc.tile_pool(name="rows_in", bufs=ROW_TILES))
        w_in = ctx.enter_context(tc.tile_pool(name="w_in", bufs=len(PIECES)))
        w_grouped = ctx.enter_context(tc.tile_pool(name="w_grouped", bufs=len(PIECES)))
        u_rows = ctx.enter_context(tc.tile_pool(name="u_rows", bufs=ROW_TILES))
        u_grouped = ctx.enter_context(tc.tile_pool(name="u_grouped", bufs=ROW_TILES))
        unread = ctx.enter_context(tc.tile_pool(name="unread", bufs=2))
        y_rows = ctx.enter_context(tc.tile_pool(name="y_rows", bufs=ROW_TILES))
        stats = ctx.enter_context(tc.tile_pool(name="stats", bufs=ROW_TILES))
        ps_t = ctx.enter_context(tc.psum_pool(name="ps_t", bufs=4))
        ps_y = ctx.enter_context(tc.psum_pool(name="ps_y", bufs=4))

        ident = const.tile([P, P], BF16, name="ident")
        ones = const.tile([P, P], BF16, name="ones")
        b_row = const.tile([P, SIZE], BF16, name="b_row")
        b_all = const.tile([P, SIZE], BF16, name="b_all")
        one = const.tile([P, 1], F32, name="one")
        warm = const.tile([P, 1], F32, name="warm")
        plus_minus = const.tile([P, 2], F32, name="plus_minus")
        half = const.tile([P, BATCH], F32, name="half")
        minus_half = const.tile([P, 1], F32, name="minus_half")
        w_codes = const.tile([P, PASSES, SIZE], U32, name="w_codes", align_bytes=64)
        w_scales = const.tile([P, PASSES, SIZE], U8, name="w_scales", align_bytes=64)
        u_codes = const.tile([P, ROW_TILES, PASSES * P], U32, name="u_codes", align_bytes=64)
        u_scales = const.tile([P, ROW_TILES, PASSES * P], U8, name="u_scales", align_bytes=64)

        mid_t = {}
        w_raw = {}
        w_grp = {}
        n_sq, n_clip, norm, inv_norm, logs, factor = {}, {}, {}, {}, {}, {}
        u_t, u_ps, u_grp = {}, {}, {}
        b_ps, y_ps = {}, {}
        y_t, m_sq, inv_m, gain = {}, {}, {}, {}

        def load_rows(i):
            mid_t[i] = rows_in.tile([P, SIZE], BF16, name="mid_t")
            nc.sync.dma_start(out=mid_t[i][:], in_=mid[i * P:(i + 1) * P, :])

        def load_w(q):
            g, h = PIECES[q]
            w_raw[q] = w_in.tile([P, PACK, BANK], BF16, name="w_raw")
            nc.sync.dma_start(
                out=w_raw[q][:],
                in_=W[g * K_PASS:(g + 1) * K_PASS, h * BANK:(h + 1) * BANK].rearrange(
                    "(t p) n -> p t n", t=PACK, p=P
                ),
            )

        def regroup_w(q):
            w_grp[q] = w_grouped.tile([P, BANK, PACK], BF16, name="w_grp", align_bytes=64)
            nc.vector.tensor_copy(
                out=w_grp[q][:].rearrange("p (c i) t -> p c t i", i=4),
                in_=w_raw[q][:].rearrange("p t (c i) -> p c t i", i=4),
            )

        def quantise_w(q):
            g, h = PIECES[q]
            nc.vector.quantize_mx(
                out=w_codes[:, g, h * BANK:(h + 1) * BANK].bitcast(FP8X4),
                scales=w_scales[:, g, h * BANK:(h + 1) * BANK],
                in_=w_grp[q][:].rearrange("p n t -> p (n t)"),
            )

        def square_sum(i):
            bt, c = divmod(i, BATCH)
            if c == 0:
                n_sq[bt] = stats.tile([P, BATCH], F32, name="n_sq")
            squares = unread.tile([P, SIZE], BF16, name="squares")
            nc.scalar.activation(out=squares[:], in_=mid_t[i][:], func=ACT.Square,
                                 accum_out=n_sq[bt][:, c:c + 1])

        def norm_root(bt):
            n_clip[bt] = stats.tile([P, BATCH], F32, name="n_clip")
            norm[bt] = stats.tile([P, BATCH], F32, name="norm")
            nc.gpsimd.tensor_scalar(out=n_clip[bt][:], in0=n_sq[bt][:],
                                    scalar1=(1.0 - EPS) * (1.0 - EPS), scalar2=EPS * EPS,
                                    op0=ALU.min, op1=ALU.max)
            nc.gpsimd.tensor_tensor(out=norm[bt][:], in0=n_clip[bt][:], in1=half[:], op=ALU.pow)

        def norm_recip(bt):
            inv_norm[bt] = stats.tile([P, BATCH], F32, name="inv_norm")
            nc.vector.reciprocal(out=inv_norm[bt][:], in_=norm[bt][:])

        def log_terms(i):
            bt, c = divmod(i, BATCH)
            if c == 0:
                logs[bt] = stats.tile([P, BATCH, 2], F32, name="logs")
            nc.scalar.activation(out=logs[bt][:, c, :], in_=plus_minus[:], func=ACT.Ln,
                                 scale=norm[bt][:, c:c + 1], bias=one[:, 0:1])

        def scale_factor(bt):
            diff = stats.tile([P, BATCH], F32, name="diff")
            factor[bt] = stats.tile([P, BATCH], F32, name="factor")
            nc.vector.tensor_tensor(out=diff[:], in0=logs[bt][:, :, 0], in1=logs[bt][:, :, 1],
                                    op=ALU.subtract)
            nc.vector.tensor_tensor(out=factor[bt][:], in0=diff[:], in1=inv_norm[bt][:],
                                    op=ALU.mult)

        def scale_rows(i):
            bt, c = divmod(i, BATCH)
            u_t[i] = u_rows.tile([P, SIZE], BF16, name="u_t")
            nc.vector.tensor_scalar(out=u_t[i][:], in0=mid_t[i][:],
                                    scalar1=factor[bt][:, c:c + 1], scalar2=0.5,
                                    op0=ALU.mult, op1=ALU.mult)

        def transpose_rows(i):
            u_ps[i] = ps_t.tile([P, PASSES, PACK, P], BF16, name="u_ps")
            for g in range(PASSES):
                for t in range(PACK):
                    first = g * K_PASS + t * P
                    nc.tensor.transpose(u_ps[i][:, g, t, :], u_t[i][:, first:first + P], ident[:])

        def regroup_rows(i):
            u_grp[i] = u_grouped.tile([P, PASSES, P, PACK], BF16, name="u_grp", align_bytes=64)
            nc.scalar.copy(out=u_grp[i][:], in_=u_ps[i][:].rearrange("p g t r -> p g r t"))

        def quantise_rows(i):
            nc.vector.quantize_mx(
                out=u_codes[:, i, :].bitcast(FP8X4),
                scales=u_scales[:, i, :],
                in_=u_grp[i][:].rearrange("p g r t -> p (g r t)"),
            )

        def multiply(i):
            for h in range(HALVES):
                y_ps[i, h] = ps_y.tile([P, BANK], F32, name="y_ps", tag="y_ps")
                for g in range(PASSES):
                    nc.tensor.matmul_mx(
                        out=y_ps[i, h][:],
                        lhsT=u_codes[:, i, g * P:(g + 1) * P].bitcast(FP8X4),
                        lhsT_scale=u_scales[:, i, g * P:(g + 1) * P],
                        rhs=w_codes[:, g, h * BANK:(h + 1) * BANK].bitcast(FP8X4),
                        rhs_scale=w_scales[:, g, h * BANK:(h + 1) * BANK],
                        start=(g == 0),
                        stop=(g == PASSES - 1),
                    )

        def add_bias(i):
            y_t[i] = y_rows.tile([P, SIZE], F32, name="y_t")
            for h in range(HALVES):
                nc.vector.tensor_tensor(out=y_t[i][:, h * BANK:(h + 1) * BANK], in0=y_ps[i, h][:],
                                        in1=b_all[:, h * BANK:(h + 1) * BANK], op=ALU.add)

        def sum_squares(i):
            products = unread.tile([P, SIZE], F32, name="products")
            total = stats.tile([P, 1], F32, name="total")
            m_sq[i] = stats.tile([P, 1], F32, name="m_sq")
            nc.vector.scalar_tensor_tensor(out=products[:], in0=y_t[i][:], scalar=0.0,
                                           in1=y_t[i][:], op0=ALU.max, op1=ALU.mult,
                                           accum_out=total[:])
            nc.vector.tensor_scalar(out=m_sq[i][:], in0=total[:], scalar1=EPS * EPS, scalar2=None,
                                    op0=ALU.max)

        def norm2_root(i):
            inv_m[i] = stats.tile([P, 1], F32, name="inv_m")
            nc.gpsimd.tensor_tensor(out=inv_m[i][:], in0=m_sq[i][:], in1=minus_half[:], op=ALU.pow)

        def out_gain(i):
            tanh_m = stats.tile([P, 1], F32, name="tanh_m")
            gain[i] = stats.tile([P, 1], F32, name="gain")
            nc.scalar.activation(out=tanh_m[:], in_=m_sq[i][:], func=ACT.Tanh, scale=inv_m[i][:, 0:1])
            nc.scalar.activation(out=gain[i][:], in_=tanh_m[:], func=ACT.Copy, scale=inv_m[i][:, 0:1])

        def scale_out(i):
            if i == ROW_TILES - 1:
                nc.vector.tensor_scalar(out=y_t[i][:], in0=y_t[i][:], scalar1=0.0,
                                        scalar2=gain[i][:, 0:1], op0=ALU.max, op1=ALU.mult)
            else:
                nc.scalar.activation(out=y_t[i][:], in_=y_t[i][:], func=ACT.Relu,
                                     scale=gain[i][:, 0:1])
            nc.sync.dma_start(out=out[i * P:(i + 1) * P, :], in_=y_t[i][:])

        nc.vector.memset(one[:], 1.0)
        nc.vector.memset(b_row[:], 0.0)
        nc.vector.memset(ones[:], 1.0)
        nc.gpsimd.memset(half[:], 0.5)
        nc.gpsimd.memset(minus_half[:], -0.5)
        nc.gpsimd.memset(plus_minus[:, 0:1], 1.0)
        nc.gpsimd.memset(plus_minus[:, 1:2], -1.0)
        make_identity(nc, ident[:])
        nc.scalar.dma_start(out=b_row[0:1, :], in_=b.rearrange("(o n) -> o n", o=1))
        nc.scalar.activation(out=warm[:], in_=one[:], func=ACT.Ln)

        load_rows(0)
        for q in range(len(PIECES)):
            load_rows(q + 1)
            load_w(q)
        for i in range(len(PIECES) + 1, ROW_TILES):
            load_rows(i)

        for h in range(HALVES):
            b_ps[h] = ps_y.tile([P, BANK], F32, name="b_ps", tag="y_ps")
            nc.tensor.matmul(out=b_ps[h][:], lhsT=ones[:], rhs=b_row[:, h * BANK:(h + 1) * BANK],
                             start=True, stop=True)

        for i in range(BATCH):
            square_sum(i)
        regroup_w(0)
        regroup_w(1)
        quantise_w(0)
        norm_root(0)
        for h in range(HALVES):
            nc.vector.tensor_copy(out=b_all[:, h * BANK:(h + 1) * BANK], in_=b_ps[h][:])
        norm_recip(0)
        square_sum(BATCH)
        for i in range(BATCH):
            log_terms(i)
        for i in range(BATCH + 1, ROW_TILES):
            square_sum(i)
        norm_root(1)
        regroup_w(2)
        quantise_w(1)
        scale_factor(0)
        for i in (0, 1):
            scale_rows(i)
            transpose_rows(i)
        quantise_w(2)
        regroup_w(3)
        for i in (2, 3):
            scale_rows(i)
            transpose_rows(i)
        regroup_rows(0)
        quantise_rows(0)
        quantise_w(3)
        regroup_rows(1)
        quantise_rows(1)
        regroup_rows(2)
        for i in range(BATCH, ROW_TILES):
            log_terms(i)
        regroup_rows(3)
        multiply(0)
        multiply(1)

        for i in range(ROW_TILES):
            add_bias(i)
            if i == 1:
                norm_recip(1)
                scale_factor(1)
                for later in range(BATCH, ROW_TILES):
                    scale_rows(later)
            if 1 <= i <= BATCH:
                transpose_rows(i + BATCH - 1)
                regroup_rows(i + BATCH - 1)
            sum_squares(i)
            norm2_root(i)
            if i + 2 < ROW_TILES:
                quantise_rows(i + 2)
                multiply(i + 2)
            out_gain(i)
            scale_out(i)
